import numpy as np
import ml_dtypes


def mxq(x, axis, fmt="e4m3"):
    dtype, down = {"e4m3": (ml_dtypes.float8_e4m3fn, 7), "e5m2": (ml_dtypes.float8_e5m2, 14)}[fmt]
    v = np.moveaxis(np.asarray(x, np.float32).astype(ml_dtypes.bfloat16).astype(np.float64), axis, -1)
    blocks = v.reshape(v.shape[:-1] + (-1, 32))
    amax = np.abs(blocks).max(-1, keepdims=True)
    byte = np.maximum(np.where(amax > 0, np.frexp(amax)[1] - 1 + 127, 0) - down, 1)
    scale = np.exp2(byte - 127.0)
    codes = (blocks / scale).astype(np.float32).astype(dtype).astype(np.float64)
    return np.moveaxis((codes * scale).reshape(v.shape), -1, axis)


WIDE = False


def mx_kscale(k):
    if not WIDE:
        return np.ones(k)
    levels = np.array([10, -10, 5, -5, 0])
    a = np.random.permutation(np.resize(levels, k // 512 * 4)).reshape(k // 512, 4)
    idx = np.arange(k)
    return np.exp2(a[idx // 512, idx % 128 // 32])


BF16 = ml_dtypes.bfloat16


def bf(x):
    return np.asarray(x, np.float32).astype(BF16)


def f64(x):
    return np.asarray(x).astype(np.float64)


B, I, H = 4096, 1024, 256
MXH = H % 512 == 0


def sigmoid(v):
    return 1.0 / (1.0 + np.exp(-v))


def setup_inputs():
    s = mx_kscale(I)
    u = mx_kscale(H) if MXH else np.ones(H)
    d = {"x_t": bf(np.random.standard_normal((B, I)) * s),
         "h_prev": bf(np.random.standard_normal((B, H)) * u),
         "c_prev": bf(np.random.standard_normal((B, H)))}
    for g in ("f", "i", "c", "o"):
        d["W_" + g] = bf(np.random.standard_normal((I, H)) * 0.7 / np.sqrt(I) / s[:, None])
    for g in ("f", "i", "c", "o"):
        d["U_" + g] = bf(np.random.standard_normal((H, H)) * 0.7 / np.sqrt(H) / u[:, None])
    for g in ("f", "i", "c", "o"):
        d["b_" + g] = bf(np.random.standard_normal(H) * 0.1)
    return d


def reference(x_t, h_prev, c_prev, W_f, W_i, W_c, W_o, U_f, U_i, U_c, U_o, b_f, b_i, b_c, b_o):
    W = np.concatenate([f64(W_f), f64(W_i), f64(W_c), f64(W_o)], axis=1)
    U = np.concatenate([f64(U_f), f64(U_i), f64(U_c), f64(U_o)], axis=1)
    b = np.concatenate([f64(b_f), f64(b_i), f64(b_c), f64(b_o)], axis=0)
    xw = mxq(f64(x_t), 1, "e4m3") @ mxq(W, 0, "e4m3")
    if MXH:
        hu = mxq(f64(h_prev), 1, "e4m3") @ mxq(U, 0, "e4m3")
    else:
        hu = f64(h_prev) @ U
    gates = xw + hu + b
    f_t = sigmoid(gates[:, 0 * H:1 * H])
    i_t = sigmoid(gates[:, 1 * H:2 * H])
    c_tilda_t = np.tanh(gates[:, 2 * H:3 * H])
    o_t = sigmoid(gates[:, 3 * H:4 * H])
    c_t = f_t * f64(c_prev) + i_t * c_tilda_t
    h_t = o_t * np.tanh(c_t)
    return h_t

@@ -1,0 +1,322 @@
+from contextlib import ExitStack
+
+import concourse.mybir as mybir
+from concourse.masks import make_identity
+
+F32 = mybir.dt.float32
+BF16 = mybir.dt.bfloat16
+U32 = mybir.dt.uint32
+U8 = mybir.dt.uint8
+FP8X4 = mybir.dt.float8_e4m3fn_x4
+ACT = mybir.ActivationFunctionType
+ALU = mybir.AluOpType
+
+P = 128
+BATCH, IN, HID = 4096, 1024, 256
+GATES = 4 * HID
+HALF = 512
+NT = BATCH // P
+NPAIR = NT // 2
+FLOPS = 2 * BATCH * GATES * (IN + HID)
+
+BIAS_MM = ()
+D_ON_V = tuple(range(NPAIR - 2, NPAIR))
+P4_ON_V = tuple(range(NPAIR - 1, NPAIR))
+REGROUP = ("v", "v", "v", "v", "s", "s", "v", "v")
+LEAD_HU = 2
+LEAD_TR, LEAD_EXIT, LEAD_Q = 3, 2, 1
+XC_BUFS, XG_BUFS = 3, 3
+GT_BUFS = 5
+TR_BANKS, HU_BANKS, XW_BANKS = 4, 2, 2
+OUT_LAG = 1
+LOADS = (
+    ("w", 0, 0), ("w", 1, 0), ("h", 0, 8), ("u", 0, 0), ("x", 0, 2), ("w", 2, 0), ("w", 3, 0), ("x", 2, 4),
+    ("c", 0, 8), ("x", 4, 8), ("h", 8, 32), ("x", 8, 12), ("c", 8, 32), ("x", 12, 16), ("x", 16, 20),
+    ("x", 20, 24), ("x", 24, 28), ("x", 28, 32),
+)
+W_AT = ((-4, (0, 1, 2, 3)), (-1, (4, 5, 6, 7)))
+
+
+def tile_lstmcell_t_kernel(
+    tc, x_t, h_prev, c_prev, W_f, W_i, W_c, W_o, U_f, U_i, U_c, U_o, b_f, b_i, b_c, b_o, out
+):
+    nc = tc.nc
+    w_in = (W_f, W_i, W_o, W_c)
+    u_in = (U_f, U_i, U_o, U_c)
+    b_in = (b_f, b_i, b_o, b_c)
+    xv = x_t.rearrange("(p t) k -> p t k", t=NT)
+    hv = h_prev.rearrange("(p t) k -> p t k", t=NT)
+    cv = c_prev.rearrange("(p t) k -> p t k", t=NT)
+    ov = out.rearrange("(p t) j -> p t j", t=NT)
+
+    with ExitStack() as es:
+        keep = es.enter_context(tc.tile_pool(name="keep", bufs=1))
+        wgp = es.enter_context(tc.tile_pool(name="wgp", bufs=4))
+        xgp = es.enter_context(tc.tile_pool(name="xgp", bufs=XG_BUFS))
+        xcp = es.enter_context(tc.tile_pool(name="xcp", bufs=XC_BUFS))
+        htp = es.enter_context(tc.tile_pool(name="htp", bufs=3))
+        gtp = es.enter_context(tc.tile_pool(name="gtp", bufs=GT_BUFS))
+        p4p = es.enter_context(tc.tile_pool(name="p4p", bufs=3))
+        outp = es.enter_context(tc.tile_pool(name="outp", bufs=4))
+        ps_tr = es.enter_context(tc.psum_pool(name="ps_tr", bufs=TR_BANKS))
+        ps_hu = es.enter_context(tc.psum_pool(name="ps_hu", bufs=HU_BANKS))
+        ps_xw = es.enter_context(tc.psum_pool(name="ps_xw", bufs=XW_BANKS))
+        es.enter_context(tc.manual_schedule())
+
+        ident = keep.tile([P, P], F32, name="ident")
+        ones = keep.tile([P, P], BF16, name="ones")
+        bpad = keep.tile([P, GATES], BF16, name="bpad")
+        bias_bc = keep.tile([P, GATES], F32, name="bias_bc")
+        warm_in = keep.tile([P, 1], F32, name="warm_in")
+        warm_out = keep.tile([P, 1], F32, name="warm_out")
+        usb = keep.tile([P, 4, 2, HID], BF16, name="usb")
+        wraw = keep.tile([P, 4, 2 * IN], BF16, name="wraw")
+        wc = keep.tile([P, 2, GATES], U32, name="wc", align_bytes=64)
+        wsc = keep.tile([P, 2, GATES], U8, name="wsc", align_bytes=64)
+        hs = keep.tile([P, NT, HID], BF16, name="hs")
+        cs = keep.tile([P, NT, HID], BF16, name="cs")
+        xs = [keep.tile([P, 4, IN], BF16, name="xs%d" % c) for c in range(NT // 4)]
+
+        nc.vector.memset(bpad[:], 0.0)
+        nc.vector.memset(ones[:], 1.0)
+        nc.vector.memset(warm_in[:], 0.0)
+        for pos in range(4):
+            nc.scalar.dma_start(
+                out=bpad[0:1, pos * HID : (pos + 1) * HID], in_=b_in[pos].rearrange("(o c) -> o c", o=1)
+            )
+        nc.scalar.activation(out=warm_out[:], in_=warm_in[:], func=ACT.Sigmoid)
+        make_identity(nc, ident[:])
+
+        def load_w(pos):
+            nc.sync.dma_start(
+                out=wraw[:, pos, :].rearrange("p (j r) -> p j r", j=4),
+                in_=w_in[pos].rearrange("(j q e) c -> q j (e c)", j=4, q=P, e=2),
+            )
+
+        def load_u():
+            for pos in range(4):
+                nc.sync.dma_start(out=usb[:, pos, :, :], in_=u_in[pos].rearrange("(q e) c -> q e c", e=2))
+
+        def load_rows(dst, view, lo, hi):
+            nc.sync.dma_start(out=dst[:, lo:hi, :], in_=view[:, lo:hi, :])
+
+        def load_x(lo, hi):
+            nc.sync.dma_start(out=xs[lo // 4][:, lo % 4 : lo % 4 + hi - lo, :], in_=xv[:, lo:hi, :])
+
+        for kind, lo, hi in LOADS:
+            if kind == "w":
+                load_w(lo)
+            elif kind == "u":
+                load_u()
+            elif kind == "h":
+                load_rows(hs, hv, lo, hi)
+            elif kind == "c":
+                load_rows(cs, cv, lo, hi)
+            else:
+                load_x(lo, hi)
+
+        trx, xg, xc, xsc, trh, hT, hu, xw, gt, ta, tb, ot = {}, {}, {}, {}, {}, {}, {}, {}, {}, {}, {}, {}
+
+        def x_transposes(t):
+            trx[t] = ps_tr.tile([P, 4, P], F32, name="tr")
+            words = xs[t // 4][:, t % 4, :].bitcast(F32)
+            return [
+                lambda j=j: nc.tensor.transpose(out=trx[t][:, j, :], in_=words[:, j * P : (j + 1) * P], identity=ident[:])
+                for j in range(4)
+            ]
+
+        def x_exit(t):
+            xg[t] = xgp.tile([P, IN], BF16, name="xg", align_bytes=64)
+            nc.scalar.copy(
+                out=xg[t][:].bitcast(F32).rearrange("p (g b u) -> p g b u", g=2, u=2),
+                in_=trx[t][:].rearrange("p (g u) b -> p g b u", g=2),
+            )
+
+        def x_quant(t):
+            xc[t] = xcp.tile([P, 2 * P], U32, name="xc", align_bytes=64)
+            xsc[t] = xcp.tile([P, 2 * P], U8, name="xsc", align_bytes=64)
+            nc.vector.quantize_mx(out=xc[t][:].bitcast(FP8X4), scales=xsc[t][:], in_=xg[t][:])
+
+        def h_transposes(q, which):
+            if q not in trh:
+                trh[q] = ps_tr.tile([P, 4, P], F32, name="tr")
+            return [
+                lambda i=i: nc.tensor.transpose(
+                    out=trh[q][:, i, :], in_=hs[:, 4 * q + i, :].bitcast(F32), identity=ident[:]
+                )
+                for i in which
+            ]
+
+        def h_exit(q):
+            hT[q] = htp.tile([P, 4, P], F32, name="hT")
+            nc.scalar.copy(out=hT[q][:], in_=trh[q][:])
+
+        def hu_matmuls(t):
+            lhs = hT[t // 4][:, t % 4, :].bitcast(BF16).rearrange("p (b e) -> p b e", e=2)
+            with_bias = t in BIAS_MM
+            mms = []
+            for half in range(2):
+                hu[(t, half)] = ps_hu.tile([P, HALF], F32, name="hu")
+                cols = slice(half * HALF, (half + 1) * HALF)
+                if with_bias:
+                    mms.append(
+                        lambda half=half, cols=cols: nc.tensor.matmul(
+                            out=hu[(t, half)][:], lhsT=ones[:], rhs=bpad[:, cols], start=True, stop=False
+                        )
+                    )
+                for e in range(2):
+                    mms.append(
+                        lambda half=half, cols=cols, e=e: nc.tensor.matmul(
+                            out=hu[(t, half)][:].rearrange("p (a c) -> p a c", a=2),
+                            lhsT=lhs[:, :, e],
+                            rhs=usb[:, 2 * half : 2 * half + 2, e, :],
+                            start=(e == 0 and not with_bias),
+                            stop=(e == 1),
+                        )
+                    )
+            return mms
+
+        def weave(mms, trs):
+            if not mms:
+                for tr in trs:
+                    tr()
+                return
+            k = 0
+            gaps = len(mms) - 1
+            for i, mm in enumerate(mms):
+                mm()
+                if i < gaps:
+                    share = -((k - len(trs)) // (gaps - i))
+                    for tr in trs[k : k + share]:
+                        tr()
+                    k += share
+
+        def gate_view(t, cols):
+            return gt[t // 2][:, t % 2, cols]
+
+        def hu_exit(t):
+            if t % 2 == 0:
+                gt[t // 2] = gtp.tile([P, 2, GATES], F32, name="gt")
+            for half in range(2):
+                cols = slice(half * HALF, (half + 1) * HALF)
+                if t in BIAS_MM:
+                    nc.scalar.copy(out=gate_view(t, cols), in_=hu[(t, half)][:])
+                else:
+                    nc.vector.tensor_tensor(
+                        out=gate_view(t, cols), in0=hu[(t, half)][:], in1=bias_bc[:, cols], op=ALU.add
+                    )
+
+        def mx_passes(t):
+            for half in range(2):
+                xw[(t, half)] = ps_xw.tile([P, HALF], F32, name="xw")
+                cols = slice(half * HALF, (half + 1) * HALF)
+                for g in range(2):
+                    rows = slice(g * P, (g + 1) * P)
+                    nc.tensor.matmul_mx(
+                        out=xw[(t, half)][:],
+                        lhsT=xc[t][:, rows].bitcast(FP8X4),
+                        lhsT_scale=xsc[t][:, rows],
+                        rhs=wc[:, g, cols].bitcast(FP8X4),
+                        rhs_scale=wsc[:, g, cols],
+                        start=(g == 0),
+                        stop=(g == 1),
+                    )
+
+        def add_xw(t):
+            for half in range(2):
+                cols = slice(half * HALF, (half + 1) * HALF)
+                nc.vector.tensor_tensor(
+                    out=gate_view(t, cols), in0=xw[(t, half)][:], in1=gate_view(t, cols), op=ALU.add
+                )
+
+        def gate_functions(t):
+            sig = gate_view(t, slice(0, 3 * HID))
+            tnh = gate_view(t, slice(3 * HID, GATES))
+            nc.scalar.activation(out=sig, in_=sig, func=ACT.Sigmoid)
+            nc.scalar.activation(out=tnh, in_=tnh, func=ACT.Tanh)
+
+        def cell_update(j):
+            eng = nc.vector if j in P4_ON_V else nc.gpsimd
+            g = gt[j]
+            ta[j] = p4p.tile([P, 2, HID], F32, name="ta")
+            tb[j] = p4p.tile([P, 2, HID], F32, name="tb")
+            eng.tensor_tensor(out=ta[j][:], in0=g[:, :, 0:HID], in1=cs[:, 2 * j : 2 * j + 2, :], op=ALU.mult)
+            eng.tensor_tensor(out=tb[j][:], in0=g[:, :, HID : 2 * HID], in1=g[:, :, 3 * HID : GATES], op=ALU.mult)
+            eng.tensor_tensor(out=ta[j][:], in0=ta[j][:], in1=tb[j][:], op=ALU.add)
+
+        def cell_tanh(j):
+            nc.scalar.activation(out=ta[j][:], in_=ta[j][:], func=ACT.Tanh)
+
+        def output(j):
+            eng = nc.vector if (j in D_ON_V or j in P4_ON_V) else nc.gpsimd
+            ot[j] = outp.tile([P, 2, HID], F32, name="ot")
+            eng.tensor_tensor(out=ot[j][:], in0=gt[j][:, :, 2 * HID : 3 * HID], in1=ta[j][:], op=ALU.mult)
+            nc.sync.dma_start(out=ov[:, 2 * j : 2 * j + 2, :], in_=ot[j][:])
+
+        def w_piece(n):
+            pos, g = n // 2, n % 2
+            wg = wgp.tile([P, IN], BF16, name="wg", align_bytes=64)
+            src = wraw[:, pos, g * IN : (g + 1) * IN].rearrange("p (t c i) -> p c t i", t=4, i=4)
+            dst = wg[:].rearrange("p (c i t) -> p c t i", i=4, t=4)
+            if REGROUP[n] == "v":
+                nc.vector.tensor_copy(out=dst, in_=src)
+            elif REGROUP[n] == "s":
+                nc.scalar.copy(out=dst, in_=src)
+            else:
+                nc.gpsimd.tensor_scalar(out=dst, in0=src, scalar1=1.0, scalar2=0.0, op0=ALU.mult, op1=ALU.add)
+            return wg
+
+        def w_quant(n, wg):
+            pos, g = n // 2, n % 2
+            cols = slice(pos * HID, (pos + 1) * HID)
+            nc.vector.quantize_mx(out=wc[:, g, cols].bitcast(FP8X4), scales=wsc[:, g, cols], in_=wg[:])
+
+        for half in range(2):
+            cols = slice(half * HALF, (half + 1) * HALF)
+            bb = ps_hu.tile([P, HALF], F32, name="hu")
+            nc.tensor.matmul(out=bb[:], lhsT=ones[:], rhs=bpad[:, cols], start=True, stop=True)
+            nc.scalar.copy(out=bias_bc[:, cols], in_=bb[:])
+        weave([], h_transposes(0, range(4)))
+        h_exit(0)
+
+        w_at = dict(W_AT)
+
+        for s in range(-8, NT + 8):
+            trs = []
+            if 0 <= s + LEAD_TR < NT:
+                trs += x_transposes(s + LEAD_TR)
+            for q in range(1, NT // 4):
+                if s == 4 * q - LEAD_HU - 4:
+                    trs += h_transposes(q, (0, 1))
+                if s == 4 * q - LEAD_HU - 3:
+                    trs += h_transposes(q, (2, 3))
+            mms = hu_matmuls(s + LEAD_HU) if 0 <= s + LEAD_HU < NT else []
+            weave(mms, trs)
+            pieces = [(n, w_piece(n)) for n in w_at.get(s, ())]
+            for n, wg in pieces:
+                w_quant(n, wg)
+            if 0 <= s < NT:
+                mx_passes(s)
+            if 0 <= s + LEAD_EXIT < NT:
+                x_exit(s + LEAD_EXIT)
+            if 0 <= s - 1 < NT:
+                gate_functions(s - 1)
+            for q in range(1, NT // 4):
+                if s == 4 * q - LEAD_HU - 2:
+                    h_exit(q)
+            if 0 <= s + LEAD_HU < NT:
+                hu_exit(s + LEAD_HU)
+            if 0 <= s < NT:
+                add_xw(s)
+            if 0 <= s + LEAD_Q < NT:
+                x_quant(s + LEAD_Q)
+            if s % 2 == 0:
+                j = (s - 2) // 2
+                if 0 <= j - 1 < NPAIR:
+                    cell_tanh(j - 1)
+                if 0 <= j < NPAIR:
+                    cell_update(j)
+            if (s - OUT_LAG) % 2 == 0:
+                j = (s - OUT_LAG - 2) // 2
+                if 0 <= j - 1 < NPAIR:
+                    output(j - 1)

@@ -19,22 +19,28 @@ NT = BATCH // P
 NPAIR = NT // 2
 FLOPS = 2 * BATCH * GATES * (IN + HID)
 
-BIAS_MM = ()
-D_ON_V = tuple(range(NPAIR - 2, NPAIR))
-P4_ON_V = tuple(range(NPAIR - 1, NPAIR))
-REGROUP = ("v", "v", "v", "v", "s", "s", "v", "v")
-LEAD_HU = 2
-LEAD_TR, LEAD_EXIT, LEAD_Q = 3, 2, 1
-XC_BUFS, XG_BUFS = 3, 3
-GT_BUFS = 5
-TR_BANKS, HU_BANKS, XW_BANKS = 4, 2, 2
-OUT_LAG = 1
+S_HALVES = tuple([(t, h) for t in range(4) for h in range(2)] + [(t, 1) for t in range(5, 30, 2)])
+G_OPS = 3
+V_PAIRS = (NPAIR - 1,)
+LH_STEPS = (8, 16, 24)
+LX = 3
+TAIL = {"cell": 1.0, "next": 0.1, "O": 0.15}
+
+
+def lead(t):
+    return 4 - len([step for step in LH_STEPS if t >= step])
+BUFS = {"tr": 2, "hu": 3, "xw": 3, "xg": 2, "xc": 2, "hT": 2, "gt": 6, "ta": 3, "tb": 2, "ot": 3, "wg": 2}
 LOADS = (
-    ("w", 0, 0), ("w", 1, 0), ("h", 0, 8), ("u", 0, 0), ("x", 0, 2), ("w", 2, 0), ("w", 3, 0), ("x", 2, 4),
-    ("c", 0, 8), ("x", 4, 8), ("h", 8, 32), ("x", 8, 12), ("c", 8, 32), ("x", 12, 16), ("x", 16, 20),
+    ("u", 0, 0), ("h", 0, 4), ("w", 0, 0), ("w", 1, 0), ("x", 0, 2), ("w", 2, 0), ("w", 3, 0), ("x", 2, 4),
+    ("h", 4, 8), ("c", 0, 8), ("x", 4, 8), ("h", 8, 32), ("x", 8, 12), ("c", 8, 32), ("x", 12, 16), ("x", 16, 20),
     ("x", 20, 24), ("x", 24, 28), ("x", 28, 32),
 )
-W_AT = ((-4, (0, 1, 2, 3)), (-1, (4, 5, 6, 7)))
+W_ENG = ("v", "v", "v", "v", "v", "v", "v", "v")
+VT = {
+    "WR": (-3.9, -2.9), "WQ": (-3.5, -2.5), "BB": -5.0, "TRH": -1.6, "HE": -1.3,
+    "XE": 0.35, "CS": 0.5, "ACT0": 0.75, "ACT1": 0.97, "TC": 4.4,
+    "C": 0.3, "D": 0.6, "Q": -0.06, "O": 5.96, "CELL": 1.99,
+}
 
 
 def tile_lstmcell_t_kernel(
@@ -51,16 +57,8 @@ def tile_lstmcell_t_kernel(
 
     with ExitStack() as es:
         keep = es.enter_context(tc.tile_pool(name="keep", bufs=1))
-        wgp = es.enter_context(tc.tile_pool(name="wgp", bufs=4))
-        xgp = es.enter_context(tc.tile_pool(name="xgp", bufs=XG_BUFS))
-        xcp = es.enter_context(tc.tile_pool(name="xcp", bufs=XC_BUFS))
-        htp = es.enter_context(tc.tile_pool(name="htp", bufs=3))
-        gtp = es.enter_context(tc.tile_pool(name="gtp", bufs=GT_BUFS))
-        p4p = es.enter_context(tc.tile_pool(name="p4p", bufs=3))
-        outp = es.enter_context(tc.tile_pool(name="outp", bufs=4))
-        ps_tr = es.enter_context(tc.psum_pool(name="ps_tr", bufs=TR_BANKS))
-        ps_hu = es.enter_context(tc.psum_pool(name="ps_hu", bufs=HU_BANKS))
-        ps_xw = es.enter_context(tc.psum_pool(name="ps_xw", bufs=XW_BANKS))
+        work = es.enter_context(tc.tile_pool(name="work", bufs=1))
+        psum = es.enter_context(tc.psum_pool(name="psum", bufs=1))
         es.enter_context(tc.manual_schedule())
 
         ident = keep.tile([P, P], F32, name="ident")
@@ -71,8 +69,8 @@ def tile_lstmcell_t_kernel(
         warm_out = keep.tile([P, 1], F32, name="warm_out")
         usb = keep.tile([P, 4, 2, HID], BF16, name="usb")
         wraw = keep.tile([P, 4, 2 * IN], BF16, name="wraw")
-        wc = keep.tile([P, 2, GATES], U32, name="wc", align_bytes=64)
-        wsc = keep.tile([P, 2, GATES], U8, name="wsc", align_bytes=64)
+        wc = keep.tile([P, 2, 2, HALF], U32, name="wc", align_bytes=64)
+        wsc = keep.tile([P, 2, 2, HALF], U8, name="wsc", align_bytes=64)
         hs = keep.tile([P, NT, HID], BF16, name="hs")
         cs = keep.tile([P, NT, HID], BF16, name="cs")
         xs = [keep.tile([P, 4, IN], BF16, name="xs%d" % c) for c in range(NT // 4)]
@@ -87,236 +85,286 @@ def tile_lstmcell_t_kernel(
         nc.scalar.activation(out=warm_out[:], in_=warm_in[:], func=ACT.Sigmoid)
         make_identity(nc, ident[:])
 
-        def load_w(pos):
-            nc.sync.dma_start(
-                out=wraw[:, pos, :].rearrange("p (j r) -> p j r", j=4),
-                in_=w_in[pos].rearrange("(j q e) c -> q j (e c)", j=4, q=P, e=2),
-            )
-
-        def load_u():
-            for pos in range(4):
-                nc.sync.dma_start(out=usb[:, pos, :, :], in_=u_in[pos].rearrange("(q e) c -> q e c", e=2))
-
-        def load_rows(dst, view, lo, hi):
-            nc.sync.dma_start(out=dst[:, lo:hi, :], in_=view[:, lo:hi, :])
-
-        def load_x(lo, hi):
-            nc.sync.dma_start(out=xs[lo // 4][:, lo % 4 : lo % 4 + hi - lo, :], in_=xv[:, lo:hi, :])
-
         for kind, lo, hi in LOADS:
             if kind == "w":
-                load_w(lo)
-            elif kind == "u":
-                load_u()
-            elif kind == "h":
-                load_rows(hs, hv, lo, hi)
-            elif kind == "c":
-                load_rows(cs, cv, lo, hi)
-            else:
-                load_x(lo, hi)
-
-        trx, xg, xc, xsc, trh, hT, hu, xw, gt, ta, tb, ot = {}, {}, {}, {}, {}, {}, {}, {}, {}, {}, {}, {}
-
-        def x_transposes(t):
-            trx[t] = ps_tr.tile([P, 4, P], F32, name="tr")
-            words = xs[t // 4][:, t % 4, :].bitcast(F32)
-            return [
-                lambda j=j: nc.tensor.transpose(out=trx[t][:, j, :], in_=words[:, j * P : (j + 1) * P], identity=ident[:])
-                for j in range(4)
-            ]
-
-        def x_exit(t):
-            xg[t] = xgp.tile([P, IN], BF16, name="xg", align_bytes=64)
-            nc.scalar.copy(
-                out=xg[t][:].bitcast(F32).rearrange("p (g b u) -> p g b u", g=2, u=2),
-                in_=trx[t][:].rearrange("p (g u) b -> p g b u", g=2),
-            )
-
-        def x_quant(t):
-            xc[t] = xcp.tile([P, 2 * P], U32, name="xc", align_bytes=64)
-            xsc[t] = xcp.tile([P, 2 * P], U8, name="xsc", align_bytes=64)
-            nc.vector.quantize_mx(out=xc[t][:].bitcast(FP8X4), scales=xsc[t][:], in_=xg[t][:])
-
-        def h_transposes(q, which):
-            if q not in trh:
-                trh[q] = ps_tr.tile([P, 4, P], F32, name="tr")
-            return [
-                lambda i=i: nc.tensor.transpose(
-                    out=trh[q][:, i, :], in_=hs[:, 4 * q + i, :].bitcast(F32), identity=ident[:]
+                nc.sync.dma_start(
+                    out=wraw[:, lo, :].rearrange("p (j r) -> p j r", j=4),
+                    in_=w_in[lo].rearrange("(j q e) c -> q j (e c)", j=4, q=P, e=2),
                 )
-                for i in which
-            ]
+            elif kind == "u":
+                for pos in range(4):
+                    nc.sync.dma_start(out=usb[:, pos, :, :], in_=u_in[pos].rearrange("(q e) c -> q e c", e=2))
+            elif kind == "h":
+                nc.sync.dma_start(out=hs[:, lo:hi, :], in_=hv[:, lo:hi, :])
+            elif kind == "c":
+                nc.sync.dma_start(out=cs[:, lo:hi, :], in_=cv[:, lo:hi, :])
+            else:
+                nc.sync.dma_start(out=xs[lo // 4][:, lo % 4 : lo % 4 + hi - lo, :], in_=xv[:, lo:hi, :])
 
-        def h_exit(q):
-            hT[q] = htp.tile([P, 4, P], F32, name="hT")
-            nc.scalar.copy(out=hT[q][:], in_=trh[q][:])
+        tiles = {}
+        queue = {"t": [], "s": [], "v": [], "g": []}
 
-        def hu_matmuls(t):
-            lhs = hT[t // 4][:, t % 4, :].bitcast(BF16).rearrange("p (b e) -> p b e", e=2)
-            with_bias = t in BIAS_MM
-            mms = []
-            for half in range(2):
-                hu[(t, half)] = ps_hu.tile([P, HALF], F32, name="hu")
-                cols = slice(half * HALF, (half + 1) * HALF)
-                if with_bias:
-                    mms.append(
-                        lambda half=half, cols=cols: nc.tensor.matmul(
-                            out=hu[(t, half)][:], lhsT=ones[:], rhs=bpad[:, cols], start=True, stop=False
-                        )
-                    )
-                for e in range(2):
-                    mms.append(
-                        lambda half=half, cols=cols, e=e: nc.tensor.matmul(
-                            out=hu[(t, half)][:].rearrange("p (a c) -> p a c", a=2),
-                            lhsT=lhs[:, :, e],
-                            rhs=usb[:, 2 * half : 2 * half + 2, e, :],
-                            start=(e == 0 and not with_bias),
-                            stop=(e == 1),
-                        )
-                    )
-            return mms
+        def put(engine, when, key, needs, emit, alloc=()):
+            queue[engine].append((when, len(queue[engine]), key, list(needs), emit, alloc))
 
-        def weave(mms, trs):
-            if not mms:
-                for tr in trs:
-                    tr()
-                return
-            k = 0
-            gaps = len(mms) - 1
-            for i, mm in enumerate(mms):
-                mm()
-                if i < gaps:
-                    share = -((k - len(trs)) // (gaps - i))
-                    for tr in trs[k : k + share]:
-                        tr()
-                    k += share
+        def sb(tag, key, shape, dtype):
+            tiles[key] = work.tile(shape, dtype, name=tag, bufs=BUFS[tag], align_bytes=64)
+
+        def ps(tag, key, shape):
+            tiles[key] = psum.tile(shape, F32, name=tag, bufs=BUFS[tag])
+
+        def cols_of(half):
+            return slice(half * HALF, (half + 1) * HALF)
 
         def gate_view(t, cols):
-            return gt[t // 2][:, t % 2, cols]
+            return tiles[("gt", t // 2)][:, t % 2, cols]
 
-        def hu_exit(t):
-            if t % 2 == 0:
-                gt[t // 2] = gtp.tile([P, 2, GATES], F32, name="gt")
-            for half in range(2):
-                cols = slice(half * HALF, (half + 1) * HALF)
-                if t in BIAS_MM:
-                    nc.scalar.copy(out=gate_view(t, cols), in_=hu[(t, half)][:])
-                else:
-                    nc.vector.tensor_tensor(
-                        out=gate_view(t, cols), in0=hu[(t, half)][:], in1=bias_bc[:, cols], op=ALU.add
-                    )
+        def bias_matmul(half):
+            ps("hu", ("bb", half), [P, HALF])
+            nc.tensor.matmul(out=tiles[("bb", half)][:], lhsT=ones[:], rhs=bpad[:, cols_of(half)], start=True, stop=True)
 
-        def mx_passes(t):
-            for half in range(2):
-                xw[(t, half)] = ps_xw.tile([P, HALF], F32, name="xw")
-                cols = slice(half * HALF, (half + 1) * HALF)
-                for g in range(2):
-                    rows = slice(g * P, (g + 1) * P)
-                    nc.tensor.matmul_mx(
-                        out=xw[(t, half)][:],
-                        lhsT=xc[t][:, rows].bitcast(FP8X4),
-                        lhsT_scale=xsc[t][:, rows],
-                        rhs=wc[:, g, cols].bitcast(FP8X4),
-                        rhs_scale=wsc[:, g, cols],
-                        start=(g == 0),
-                        stop=(g == 1),
-                    )
-
-        def add_xw(t):
-            for half in range(2):
-                cols = slice(half * HALF, (half + 1) * HALF)
-                nc.vector.tensor_tensor(
-                    out=gate_view(t, cols), in0=xw[(t, half)][:], in1=gate_view(t, cols), op=ALU.add
-                )
-
-        def gate_functions(t):
-            sig = gate_view(t, slice(0, 3 * HID))
-            tnh = gate_view(t, slice(3 * HID, GATES))
-            nc.scalar.activation(out=sig, in_=sig, func=ACT.Sigmoid)
-            nc.scalar.activation(out=tnh, in_=tnh, func=ACT.Tanh)
-
-        def cell_update(j):
-            eng = nc.vector if j in P4_ON_V else nc.gpsimd
-            g = gt[j]
-            ta[j] = p4p.tile([P, 2, HID], F32, name="ta")
-            tb[j] = p4p.tile([P, 2, HID], F32, name="tb")
-            eng.tensor_tensor(out=ta[j][:], in0=g[:, :, 0:HID], in1=cs[:, 2 * j : 2 * j + 2, :], op=ALU.mult)
-            eng.tensor_tensor(out=tb[j][:], in0=g[:, :, HID : 2 * HID], in1=g[:, :, 3 * HID : GATES], op=ALU.mult)
-            eng.tensor_tensor(out=ta[j][:], in0=ta[j][:], in1=tb[j][:], op=ALU.add)
-
-        def cell_tanh(j):
-            nc.scalar.activation(out=ta[j][:], in_=ta[j][:], func=ACT.Tanh)
-
-        def output(j):
-            eng = nc.vector if (j in D_ON_V or j in P4_ON_V) else nc.gpsimd
-            ot[j] = outp.tile([P, 2, HID], F32, name="ot")
-            eng.tensor_tensor(out=ot[j][:], in0=gt[j][:, :, 2 * HID : 3 * HID], in1=ta[j][:], op=ALU.mult)
-            nc.sync.dma_start(out=ov[:, 2 * j : 2 * j + 2, :], in_=ot[j][:])
-
-        def w_piece(n):
-            pos, g = n // 2, n % 2
-            wg = wgp.tile([P, IN], BF16, name="wg", align_bytes=64)
-            src = wraw[:, pos, g * IN : (g + 1) * IN].rearrange("p (t c i) -> p c t i", t=4, i=4)
-            dst = wg[:].rearrange("p (c i t) -> p c t i", i=4, t=4)
-            if REGROUP[n] == "v":
-                nc.vector.tensor_copy(out=dst, in_=src)
-            elif REGROUP[n] == "s":
-                nc.scalar.copy(out=dst, in_=src)
-            else:
-                nc.gpsimd.tensor_scalar(out=dst, in0=src, scalar1=1.0, scalar2=0.0, op0=ALU.mult, op1=ALU.add)
-            return wg
-
-        def w_quant(n, wg):
-            pos, g = n // 2, n % 2
-            cols = slice(pos * HID, (pos + 1) * HID)
-            nc.vector.quantize_mx(out=wc[:, g, cols].bitcast(FP8X4), scales=wsc[:, g, cols], in_=wg[:])
+        def bias_exit(half):
+            nc.scalar.copy(out=bias_bc[:, cols_of(half)], in_=tiles[("bb", half)][:])
 
         for half in range(2):
-            cols = slice(half * HALF, (half + 1) * HALF)
-            bb = ps_hu.tile([P, HALF], F32, name="hu")
-            nc.tensor.matmul(out=bb[:], lhsT=ones[:], rhs=bpad[:, cols], start=True, stop=True)
-            nc.scalar.copy(out=bias_bc[:, cols], in_=bb[:])
-        weave([], h_transposes(0, range(4)))
-        h_exit(0)
+            put("t", VT["BB"], ("BB", half), (), lambda half=half: bias_matmul(half), (("hu", ("BBX", half)),))
+            put("s", VT["BB"], ("BBX", half), (("BB", half),), lambda half=half: bias_exit(half))
 
-        w_at = dict(W_AT)
+        def w_regroup(pos, g):
+            half, a = pos // 2, pos % 2
+            if a == 0:
+                sb("wg", ("wg", half, g), [P, 4 * HALF], BF16)
+            src = wraw[:, pos, g * IN : (g + 1) * IN].rearrange("p (t c i) -> p c t i", t=4, i=4)
+            dst = tiles[("wg", half, g)][:, a * IN : (a + 1) * IN].rearrange("p (c i t) -> p c t i", i=4, t=4)
+            if W_ENG[2 * pos + g] == "v":
+                nc.vector.tensor_copy(out=dst, in_=src)
+            else:
+                nc.scalar.copy(out=dst, in_=src)
 
-        for s in range(-8, NT + 8):
-            trs = []
-            if 0 <= s + LEAD_TR < NT:
-                trs += x_transposes(s + LEAD_TR)
-            for q in range(1, NT // 4):
-                if s == 4 * q - LEAD_HU - 4:
-                    trs += h_transposes(q, (0, 1))
-                if s == 4 * q - LEAD_HU - 3:
-                    trs += h_transposes(q, (2, 3))
-            mms = hu_matmuls(s + LEAD_HU) if 0 <= s + LEAD_HU < NT else []
-            weave(mms, trs)
-            pieces = [(n, w_piece(n)) for n in w_at.get(s, ())]
-            for n, wg in pieces:
-                w_quant(n, wg)
-            if 0 <= s < NT:
-                mx_passes(s)
-            if 0 <= s + LEAD_EXIT < NT:
-                x_exit(s + LEAD_EXIT)
-            if 0 <= s - 1 < NT:
-                gate_functions(s - 1)
-            for q in range(1, NT // 4):
-                if s == 4 * q - LEAD_HU - 2:
-                    h_exit(q)
-            if 0 <= s + LEAD_HU < NT:
-                hu_exit(s + LEAD_HU)
-            if 0 <= s < NT:
-                add_xw(s)
-            if 0 <= s + LEAD_Q < NT:
-                x_quant(s + LEAD_Q)
-            if s % 2 == 0:
-                j = (s - 2) // 2
-                if 0 <= j - 1 < NPAIR:
-                    cell_tanh(j - 1)
-                if 0 <= j < NPAIR:
-                    cell_update(j)
-            if (s - OUT_LAG) % 2 == 0:
-                j = (s - OUT_LAG - 2) // 2
-                if 0 <= j - 1 < NPAIR:
-                    output(j - 1)
+        def w_quant(half, g):
+            nc.vector.quantize_mx(
+                out=wc[:, half, g, :].bitcast(FP8X4), scales=wsc[:, half, g, :], in_=tiles[("wg", half, g)][:]
+            )
+
+        for pos in range(4):
+            for g in range(2):
+                needs = [("WR", pos - 1, g)] if pos % 2 else ([("WQ", 0, g)] if pos == 2 else [])
+                put(
+                    W_ENG[2 * pos + g], VT["WR"][pos // 2] + 0.1 * (pos % 2) + 0.01 * g, ("WR", pos, g), needs,
+                    lambda pos=pos, g=g: w_regroup(pos, g),
+                )
+        for half in range(2):
+            for g in range(2):
+                put(
+                    "v", VT["WQ"][half] + 0.01 * g, ("WQ", half, g), (("WR", 2 * half, g), ("WR", 2 * half + 1, g)),
+                    lambda half=half, g=g: w_quant(half, g),
+                )
+
+        def h_transpose(q, i):
+            if i == 0:
+                ps("tr", ("trh", q), [P, 4, P])
+            nc.tensor.transpose(
+                out=tiles[("trh", q)][:, i, :], in_=hs[:, 4 * q + i, :].bitcast(F32), identity=ident[:]
+            )
+
+        def h_exit(q):
+            sb("hT", ("hT", q), [P, 4, P], F32)
+            nc.scalar.copy(out=tiles[("hT", q)][:], in_=tiles[("trh", q)][:])
+
+        def x_transpose(t, j):
+            if j == 0:
+                ps("tr", ("trx", t), [P, 4, P])
+            words = xs[t // 4][:, t % 4, :].bitcast(F32)
+            nc.tensor.transpose(out=tiles[("trx", t)][:, j, :], in_=words[:, j * P : (j + 1) * P], identity=ident[:])
+
+        def x_exit(t):
+            if t % 2 == 0:
+                sb("xg", ("xg", t // 2), [P, 2, IN], BF16)
+            nc.scalar.copy(
+                out=tiles[("xg", t // 2)][:, t % 2, :].bitcast(F32).rearrange("p (g b u) -> p g b u", g=2, u=2),
+                in_=tiles[("trx", t)][:].rearrange("p (g u) b -> p g b u", g=2),
+            )
+
+        def x_quant(j):
+            sb("xc", ("xc", j), [P, 4 * P], U32)
+            tiles[("xsc", j)] = work.tile([P, 4 * P], U8, name="xsc", bufs=BUFS["xc"], align_bytes=64)
+            nc.vector.quantize_mx(
+                out=tiles[("xc", j)][:].bitcast(FP8X4),
+                scales=tiles[("xsc", j)][:],
+                in_=tiles[("xg", j)][:].rearrange("p a k -> p (a k)"),
+            )
+
+        def hu_matmul(t, half, step):
+            with_bias = (t, half) in S_HALVES
+            if step == (-1 if with_bias else 0):
+                if t % 2 == 0 and half == 0:
+                    sb("gt", ("gt", t // 2), [P, 2, GATES], F32)
+                ps("hu", ("hu", t, half), [P, HALF])
+            acc = tiles[("hu", t, half)]
+            if step < 0:
+                nc.tensor.matmul(out=acc[:], lhsT=ones[:], rhs=bpad[:, cols_of(half)], start=True, stop=False)
+            else:
+                lhs = tiles[("hT", t // 4)][:, t % 4, :].bitcast(BF16).rearrange("p (b e) -> p b e", e=2)
+                nc.tensor.matmul(
+                    out=acc[:].rearrange("p (a c) -> p a c", a=2),
+                    lhsT=lhs[:, :, step],
+                    rhs=usb[:, 2 * half : 2 * half + 2, step, :],
+                    start=(step == 0 and not with_bias),
+                    stop=(step == 1),
+                )
+
+        def hu_exit(t, half):
+            if (t, half) in S_HALVES:
+                nc.scalar.copy(out=gate_view(t, cols_of(half)), in_=tiles[("hu", t, half)][:])
+            else:
+                nc.vector.tensor_tensor(
+                    out=gate_view(t, cols_of(half)), in0=tiles[("hu", t, half)][:], in1=bias_bc[:, cols_of(half)],
+                    op=ALU.add,
+                )
+
+        def mx_pass(t, half, g):
+            if g == 0:
+                ps("xw", ("xw", t, half), [P, HALF])
+            rows = slice((2 * (t % 2) + g) * P, (2 * (t % 2) + g + 1) * P)
+            nc.tensor.matmul_mx(
+                out=tiles[("xw", t, half)][:],
+                lhsT=tiles[("xc", t // 2)][:, rows].bitcast(FP8X4),
+                lhsT_scale=tiles[("xsc", t // 2)][:, rows],
+                rhs=wc[:, half, g, :].bitcast(FP8X4),
+                rhs_scale=wsc[:, half, g, :],
+                start=(g == 0),
+                stop=(g == 1),
+            )
+
+        def add_xw(t, half):
+            view = gate_view(t, cols_of(half))
+            nc.vector.tensor_tensor(out=view, in0=tiles[("xw", t, half)][:], in1=view, op=ALU.add)
+
+        def gate_functions(t, half):
+            if half == 0:
+                view = gate_view(t, slice(0, 2 * HID))
+                nc.scalar.activation(out=view, in_=view, func=ACT.Sigmoid)
+            else:
+                view = gate_view(t, slice(2 * HID, 3 * HID))
+                nc.scalar.activation(out=view, in_=view, func=ACT.Sigmoid)
+                view = gate_view(t, slice(3 * HID, GATES))
+                nc.scalar.activation(out=view, in_=view, func=ACT.Tanh)
+
+        def cell_op(eng, j, lo, hi, n):
+            g = tiles[("gt", j)]
+            if n == 0 and lo == 0:
+                sb("ta", ("ta", j), [P, 2, HID], F32)
+            if n == 1 and lo == 0:
+                sb("tb", ("tb", j), [P, 2, HID], F32)
+            a, b = tiles[("ta", j)][:, lo:hi, :], (tiles[("tb", j)][:, lo:hi, :] if n in (1, 2) else None)
+            if n == 0:
+                eng.tensor_tensor(out=a, in0=g[:, lo:hi, 0:HID], in1=cs[:, 2 * j + lo : 2 * j + hi, :], op=ALU.mult)
+            elif n == 1:
+                eng.tensor_tensor(out=b, in0=g[:, lo:hi, HID : 2 * HID], in1=g[:, lo:hi, 3 * HID : GATES], op=ALU.mult)
+            elif n == 2:
+                eng.tensor_tensor(out=a, in0=a, in1=b, op=ALU.add)
+            elif n == 3:
+                nc.scalar.activation(out=a, in_=a, func=ACT.Tanh)
+            else:
+                if lo == 0:
+                    sb("ot", ("ot", j), [P, 2, HID], F32)
+                o = tiles[("ot", j)][:, lo:hi, :]
+                eng.tensor_tensor(out=o, in0=g[:, lo:hi, 2 * HID : 3 * HID], in1=a, op=ALU.mult)
+                nc.sync.dma_start(out=ov[:, 2 * j + lo : 2 * j + hi, :], in_=o)
+
+        for s in range(-8, NT):
+            mms, trs = [], []
+            for t in [t for t in range(NT) if t - lead(t) == s]:
+                for half in range(2):
+                    first = -1 if (t, half) in S_HALVES else 0
+                    for step in range(first, 2):
+                        alloc = ()
+                        if step == first:
+                            alloc = (("hu", ("C", t, half)),)
+                            if t % 2 == 0 and half == 0:
+                                alloc = alloc + (("gt", ("CELL", t // 2, 1, 4)),)
+                        mms.append((("H", t, half, step), (("HE", t // 4),), lambda t=t, half=half, step=step: hu_matmul(t, half, step), alloc))
+            t = s + LX
+            if 0 <= t < NT:
+                for j in range(4):
+                    trs.append((("TRX", t, j), (), lambda t=t, j=j: x_transpose(t, j), (("tr", ("XE", t)),) if j == 0 else ()))
+            for t in [t for t in range(0, NT, 4) if t - lead(t) - 2 == s]:
+                for i in range(4):
+                    trs.append((("TRH", t // 4, i), (), lambda q=t // 4, i=i: h_transpose(q, i), (("tr", ("HE", t // 4)),) if i == 0 else ()))
+            order = []
+            if not mms:
+                order = trs
+            else:
+                k, gaps = 0, len(mms) - 1
+                for i, mm in enumerate(mms):
+                    order.append(mm)
+                    if i < gaps:
+                        share = -((k - len(trs)) // (gaps - i))
+                        order.extend(trs[k : k + share])
+                        k += share
+            for key, needs, emit, alloc in order:
+                put("t", s, key, needs, emit, alloc)
+            if 0 <= s:
+                for half in range(2):
+                    for g in range(2):
+                        put(
+                            "t", s, ("M", s, half, g), (("Q", s // 2), ("WQ", half, g)),
+                            lambda s=s, half=half, g=g: mx_pass(s, half, g),
+                            (("xw", ("D", s, half)),) if g == 0 else (),
+                        )
+
+        for q in range(NT // 4):
+            put("s", 4 * q - lead(4 * q) + VT["HE"], ("HE", q), (("TRH", q, 3),), lambda q=q: h_exit(q), (("hT", ("H", 4 * q + 3, 1, 1)),))
+        for t in range(NT):
+            put("s", t - LX + VT["XE"], ("XE", t), (("TRX", t, 3),), lambda t=t: x_exit(t), (("xg", ("Q", t // 2)),) if t % 2 == 0 else ())
+            for half in range(2):
+                on_s = (t, half) in S_HALVES
+                put(
+                    "s" if on_s else "v", t - lead(t) + (VT["CS"] if on_s else VT["C"]) + 0.01 * half, ("C", t, half),
+                    (("H", t, half, 1),) + (() if on_s else (("BBX", half),)), lambda t=t, half=half: hu_exit(t, half),
+                )
+                put("v", t + VT["D"] + 0.1 * half, ("D", t, half), (("M", t, half, 1), ("C", t, half)), lambda t=t, half=half: add_xw(t, half))
+                put("s", t + (VT["ACT0"], VT["ACT1"])[half], ("ACT", t, half), (("D", t, half),), lambda t=t, half=half: gate_functions(t, half))
+        for j in range(NPAIR):
+            put("v", 2 * j + VT["Q"], ("Q", j), (("XE", 2 * j), ("XE", 2 * j + 1)), lambda j=j: x_quant(j), (("xc", ("M", 2 * j + 1, 1, 1)),))
+            parts = ((0, 1), (1, 2)) if j in V_PAIRS else ((0, 2),)
+            for lo, hi in parts:
+                last = hi - 1
+                for n in range(5):
+                    on_g = n != 3 and (n if n < 3 else 3) < G_OPS and j not in V_PAIRS
+                    engine = "s" if n == 3 else ("g" if on_g else "v")
+                    eng = nc.gpsimd if on_g else nc.vector
+                    needs = [("CELL", j, last, n - 1)] if n > 1 else []
+                    if n == 0:
+                        needs = [("ACT", 2 * j + i, 0) for i in range(lo, hi)] + ([("CELL", j - 1, 1, 0)] if j else [])
+                    if n == 1:
+                        needs = [("ACT", 2 * j + i, h) for i in range(lo, hi) for h in range(2)] + [("CELL", j, last, 0)]
+                    when = 2 * j + (VT["TC"] if n == 3 else (VT["O"] if n == 4 else VT["CELL"] + 0.001 * n))
+                    if j in V_PAIRS:
+                        when = 2 * j + 1 + TAIL["cell"] + TAIL["next"] * last + 0.001 * n + (TAIL["O"] if n == 4 else 0.0)
+                    put(engine, when, ("CELL", j, last, n), needs, lambda eng=eng, j=j, lo=lo, hi=hi, n=n: cell_op(eng, j, lo, hi, n))
+
+        rings, lists = {}, {}
+        for engine in ("t", "s", "v", "g"):
+            lists[engine] = sorted(queue[engine], key=lambda item: (item[0], item[1]))
+            for item in lists[engine]:
+                for tag, release in item[5]:
+                    ring = rings.get(tag, [])
+                    if len(ring) >= BUFS[tag]:
+                        item[3].append(ring[len(ring) - BUFS[tag]])
+                    rings[tag] = ring + [release]
+        written = set()
+        at = {"t": 0, "s": 0, "v": 0, "g": 0}
+        moved = True
+        while moved:
+            moved = False
+            for engine in ("t", "s", "v", "g"):
+                while at[engine] < len(lists[engine]) and all([k in written for k in lists[engine][at[engine]][3]]):
+                    item = lists[engine][at[engine]]
+                    item[4]()
+                    written.add(item[2])
+                    at[engine] += 1
+                    moved = True
+        assert all([at[e] == len(lists[e]) for e in at]), "the queues wait for each other: %s" % str(
+            [(lists[e][at[e]][2], [k for k in lists[e][at[e]][3] if k not in written]) for e in at if at[e] < len(lists[e])]
+        )

@@ -19,19 +19,22 @@ NT = BATCH // P
 NPAIR = NT // 2
 FLOPS = 2 * BATCH * GATES * (IN + HID)
 
-S_HALVES = tuple([(t, h) for t in range(4) for h in range(2)] + [(t, 1) for t in range(5, 30, 2)])
+S_HALVES = tuple(
+    [(t, h) for t in range(4) for h in range(2)] + [(t, 1) for t in range(5, 30, 2)] + [(t, 1) for t in range(6, 22, 4)]
+)
 G_OPS = 3
+G4_PAIRS = ()
 V_PAIRS = (NPAIR - 1,)
 LH_STEPS = (8, 16, 24)
-LX = 3
-TAIL = {"cell": 1.0, "next": 0.1, "O": 0.15}
+LX = 4
+TAIL = {"cell": 1.72, "TC": 1.99, "O": 2.73}
 
 
 def lead(t):
     return 4 - len([step for step in LH_STEPS if t >= step])
-BUFS = {"tr": 2, "hu": 3, "xw": 3, "xg": 2, "xc": 2, "hT": 2, "gt": 6, "ta": 3, "tb": 2, "ot": 3, "wg": 2}
+BUFS = {"tr": 2, "hu": 3, "xw": 3, "xg": 2, "xc": 3, "hT": 2, "gt": 6, "ta": 3, "tb": 2, "ot": 3, "wg": 2}
 LOADS = (
-    ("u", 0, 0), ("h", 0, 4), ("w", 0, 0), ("w", 1, 0), ("x", 0, 2), ("w", 2, 0), ("w", 3, 0), ("x", 2, 4),
+    ("h", 0, 4), ("u", 0, 0), ("x", 0, 2), ("w", 0, 0), ("w", 1, 0), ("x", 2, 4), ("w", 2, 0), ("w", 3, 0),
     ("h", 4, 8), ("c", 0, 8), ("x", 4, 8), ("h", 8, 32), ("x", 8, 12), ("c", 8, 32), ("x", 12, 16), ("x", 16, 20),
     ("x", 20, 24), ("x", 24, 28), ("x", 28, 32),
 )
@@ -39,7 +42,7 @@ W_ENG = ("v", "v", "v", "v", "v", "v", "v", "v")
 VT = {
     "WR": (-3.9, -2.9), "WQ": (-3.5, -2.5), "BB": -5.0, "TRH": -1.6, "HE": -1.3,
     "XE": 0.35, "CS": 0.5, "ACT0": 0.75, "ACT1": 0.97, "TC": 4.4,
-    "C": 0.3, "D": 0.6, "Q": -0.06, "O": 5.96, "CELL": 1.99,
+    "C": 0.3, "D": 0.6, "Q": -2.06, "O": 5.96, "CELL": 1.99,
 }
 
 
@@ -331,7 +334,7 @@ def tile_lstmcell_t_kernel(
             for lo, hi in parts:
                 last = hi - 1
                 for n in range(5):
-                    on_g = n != 3 and (n if n < 3 else 3) < G_OPS and j not in V_PAIRS
+                    on_g = n != 3 and ((n if n < 3 else 3) < G_OPS or j in G4_PAIRS) and j not in V_PAIRS
                     engine = "s" if n == 3 else ("g" if on_g else "v")
                     eng = nc.gpsimd if on_g else nc.vector
                     needs = [("CELL", j, last, n - 1)] if n > 1 else []
@@ -341,7 +344,7 @@ def tile_lstmcell_t_kernel(
                         needs = [("ACT", 2 * j + i, h) for i in range(lo, hi) for h in range(2)] + [("CELL", j, last, 0)]
                     when = 2 * j + (VT["TC"] if n == 3 else (VT["O"] if n == 4 else VT["CELL"] + 0.001 * n))
                     if j in V_PAIRS:
-                        when = 2 * j + 1 + TAIL["cell"] + TAIL["next"] * last + 0.001 * n + (TAIL["O"] if n == 4 else 0.0)
+                        when = 2 * j + last + (TAIL["TC"] if n == 3 else (TAIL["O"] if n == 4 else TAIL["cell"] + 0.001 * n))
                     put(engine, when, ("CELL", j, last, n), needs, lambda eng=eng, j=j, lo=lo, hi=hi, n=n: cell_op(eng, j, lo, hi, n))
 
         rings, lists = {}, {}

@@ -26,12 +26,16 @@ G_OPS = 3
 G4_PAIRS = ()
 V_PAIRS = (NPAIR - 1,)
 LH_STEPS = (8, 16, 24)
+T_ORDER = "mid"
 LX = 4
 TAIL = {"cell": 1.72, "TC": 1.99, "O": 2.73}
 
 
+LEAD0 = 4
+
+
 def lead(t):
-    return 4 - len([step for step in LH_STEPS if t >= step])
+    return LEAD0 - len([step for step in LH_STEPS if t >= step])
 BUFS = {"tr": 2, "hu": 3, "xw": 3, "xg": 2, "xc": 3, "hT": 2, "gt": 6, "ta": 3, "tb": 2, "ot": 3, "wg": 2}
 LOADS = (
     ("h", 0, 4), ("u", 0, 0), ("x", 0, 2), ("w", 0, 0), ("w", 1, 0), ("x", 2, 4), ("w", 2, 0), ("w", 3, 0),
@@ -297,6 +301,12 @@ def tile_lstmcell_t_kernel(
             order = []
             if not mms:
                 order = trs
+            elif T_ORDER == "mid":
+                order = mms[: len(mms) // 2] + trs + mms[len(mms) // 2 :]
+            elif T_ORDER == "front":
+                order = trs + mms
+            elif T_ORDER == "back":
+                order = mms + trs
             else:
                 k, gaps = 0, len(mms) - 1
                 for i, mm in enumerate(mms):

@@ -20,21 +20,30 @@ NPAIR = NT // 2
 FLOPS = 2 * BATCH * GATES * (IN + HID)
 
 S_HALVES = tuple(
-    [(t, h) for t in range(4) for h in range(2)] + [(t, 1) for t in range(5, 30, 2)] + [(t, 1) for t in range(6, 22, 4)]
+    [(t, h) for t in range(4) for h in range(2)] + [(t, 1) for t in range(5, 30, 2)] + [(t, 1) for t in range(6, 32, 4)]
 )
 G_OPS = 3
 G4_PAIRS = ()
 V_PAIRS = (NPAIR - 1,)
-LH_STEPS = (8, 16, 24)
-T_ORDER = "mid"
+LH_STEPS = (24,)
+T_ORDER = "weave"
 LX = 4
 TAIL = {"cell": 1.72, "TC": 1.99, "O": 2.73}
 
 
-LEAD0 = 4
+LEAD0 = 2
+XSLOT0 = (-3, -3, -2, -1, 1, 1, 2, 3)
+QVT0 = (-2.5, -0.5, 1.94)
+HSLOT0 = (-4, -3, -2, -1)
+
+
+def xslot(t):
+    return XSLOT0[t] if t < len(XSLOT0) else t - LX
 
 
 def lead(t):
+    if t < len(HSLOT0):
+        return t - HSLOT0[t]
     return LEAD0 - len([step for step in LH_STEPS if t >= step])
 BUFS = {"tr": 2, "hu": 3, "xw": 3, "xg": 2, "xc": 3, "hT": 2, "gt": 6, "ta": 3, "tb": 2, "ot": 3, "wg": 2}
 LOADS = (
@@ -291,8 +300,7 @@ def tile_lstmcell_t_kernel(
                             if t % 2 == 0 and half == 0:
                                 alloc = alloc + (("gt", ("CELL", t // 2, 1, 4)),)
                         mms.append((("H", t, half, step), (("HE", t // 4),), lambda t=t, half=half, step=step: hu_matmul(t, half, step), alloc))
-            t = s + LX
-            if 0 <= t < NT:
+            for t in [t for t in range(NT) if xslot(t) == s]:
                 for j in range(4):
                     trs.append((("TRX", t, j), (), lambda t=t, j=j: x_transpose(t, j), (("tr", ("XE", t)),) if j == 0 else ()))
             for t in [t for t in range(0, NT, 4) if t - lead(t) - 2 == s]:
@@ -329,7 +337,7 @@ def tile_lstmcell_t_kernel(
         for q in range(NT // 4):
             put("s", 4 * q - lead(4 * q) + VT["HE"], ("HE", q), (("TRH", q, 3),), lambda q=q: h_exit(q), (("hT", ("H", 4 * q + 3, 1, 1)),))
         for t in range(NT):
-            put("s", t - LX + VT["XE"], ("XE", t), (("TRX", t, 3),), lambda t=t: x_exit(t), (("xg", ("Q", t // 2)),) if t % 2 == 0 else ())
+            put("s", xslot(t) + VT["XE"], ("XE", t), (("TRX", t, 3),), lambda t=t: x_exit(t), (("xg", ("Q", t // 2)),) if t % 2 == 0 else ())
             for half in range(2):
                 on_s = (t, half) in S_HALVES
                 put(
@@ -339,7 +347,7 @@ def tile_lstmcell_t_kernel(
                 put("v", t + VT["D"] + 0.1 * half, ("D", t, half), (("M", t, half, 1), ("C", t, half)), lambda t=t, half=half: add_xw(t, half))
                 put("s", t + (VT["ACT0"], VT["ACT1"])[half], ("ACT", t, half), (("D", t, half),), lambda t=t, half=half: gate_functions(t, half))
         for j in range(NPAIR):
-            put("v", 2 * j + VT["Q"], ("Q", j), (("XE", 2 * j), ("XE", 2 * j + 1)), lambda j=j: x_quant(j), (("xc", ("M", 2 * j + 1, 1, 1)),))
+            put("v", QVT0[j] if j < len(QVT0) else 2 * j + VT["Q"], ("Q", j), (("XE", 2 * j), ("XE", 2 * j + 1)), lambda j=j: x_quant(j), (("xc", ("M", 2 * j + 1, 1, 1)),))
             parts = ((0, 1), (1, 2)) if j in V_PAIRS else ((0, 2),)
             for lo, hi in parts:
                 last = hi - 1

from contextlib import ExitStack

import concourse.mybir as mybir
from concourse.masks import make_identity

F32 = mybir.dt.float32
BF16 = mybir.dt.bfloat16
U32 = mybir.dt.uint32
U8 = mybir.dt.uint8
FP8X4 = mybir.dt.float8_e4m3fn_x4
ACT = mybir.ActivationFunctionType
ALU = mybir.AluOpType

P = 128
BATCH, IN, HID = 4096, 1024, 256
GATES = 4 * HID
HALF = 512
NT = BATCH // P
NPAIR = NT // 2
FLOPS = 2 * BATCH * GATES * (IN + HID)

S_HALVES = tuple(
    [(t, h) for t in range(4) for h in range(2)] + [(t, 1) for t in range(5, 30, 2)] + [(t, 1) for t in range(6, 32, 4)]
)
G_OPS = 3
G4_PAIRS = ()
V_PAIRS = (NPAIR - 1,)
LH_STEPS = (24,)
T_ORDER = "weave"
LX = 4
TAIL = {"cell": 1.72, "TC": 1.99, "O": 2.73}


LEAD0 = 2
XSLOT0 = (-3, -3, -2, -1, 1, 1, 2, 3)
QVT0 = (-2.5, -0.5, 1.94)
HSLOT0 = (-4, -3, -2, -1)


def xslot(t):
    return XSLOT0[t] if t < len(XSLOT0) else t - LX


def lead(t):
    if t < len(HSLOT0):
        return t - HSLOT0[t]
    return LEAD0 - len([step for step in LH_STEPS if t >= step])
BUFS = {"tr": 2, "hu": 3, "xw": 3, "xg": 2, "xc": 3, "hT": 2, "gt": 6, "ta": 3, "tb": 2, "ot": 3, "wg": 2}
LOADS = (
    ("h", 0, 4), ("u", 0, 0), ("x", 0, 2), ("w", 0, 0), ("w", 1, 0), ("x", 2, 4), ("w", 2, 0), ("w", 3, 0),
    ("h", 4, 8), ("c", 0, 8), ("x", 4, 8), ("h", 8, 32), ("x", 8, 12), ("c", 8, 32), ("x", 12, 16), ("x", 16, 20),
    ("x", 20, 24), ("x", 24, 28), ("x", 28, 32),
)
W_ENG = ("v", "v", "v", "v", "v", "v", "v", "v")
VT = {
    "WR": (-3.9, -2.9), "WQ": (-3.5, -2.5), "BB": -5.0, "TRH": -1.6, "HE": -1.3,
    "XE": 0.35, "CS": 0.5, "ACT0": 0.75, "ACT1": 0.97, "TC": 4.4,
    "C": 0.3, "D": 0.6, "Q": -2.06, "O": 5.96, "CELL": 1.99,
}


def tile_lstmcell_t_kernel(
    tc, x_t, h_prev, c_prev, W_f, W_i, W_c, W_o, U_f, U_i, U_c, U_o, b_f, b_i, b_c, b_o, out
):
    nc = tc.nc
    w_in = (W_f, W_i, W_o, W_c)
    u_in = (U_f, U_i, U_o, U_c)
    b_in = (b_f, b_i, b_o, b_c)
    xv = x_t.rearrange("(p t) k -> p t k", t=NT)
    hv = h_prev.rearrange("(p t) k -> p t k", t=NT)
    cv = c_prev.rearrange("(p t) k -> p t k", t=NT)
    ov = out.rearrange("(p t) j -> p t j", t=NT)

    with ExitStack() as es:
        keep = es.enter_context(tc.tile_pool(name="keep", bufs=1))
        work = es.enter_context(tc.tile_pool(name="work", bufs=1))
        psum = es.enter_context(tc.psum_pool(name="psum", bufs=1))
        es.enter_context(tc.manual_schedule())

        ident = keep.tile([P, P], F32, name="ident")
        ones = keep.tile([P, P], BF16, name="ones")
        bpad = keep.tile([P, GATES], BF16, name="bpad")
        bias_bc = keep.tile([P, GATES], F32, name="bias_bc")
        warm_in = keep.tile([P, 1], F32, name="warm_in")
        warm_out = keep.tile([P, 1], F32, name="warm_out")
        usb = keep.tile([P, 4, 2, HID], BF16, name="usb")
        wraw = keep.tile([P, 4, 2 * IN], BF16, name="wraw")
        wc = keep.tile([P, 2, 2, HALF], U32, name="wc", align_bytes=64)
        wsc = keep.tile([P, 2, 2, HALF], U8, name="wsc", align_bytes=64)
        hs = keep.tile([P, NT, HID], BF16, name="hs")
        cs = keep.tile([P, NT, HID], BF16, name="cs")
        xs = [keep.tile([P, 4, IN], BF16, name="xs%d" % c) for c in range(NT // 4)]

        nc.vector.memset(bpad[:], 0.0)
        nc.vector.memset(ones[:], 1.0)
        nc.vector.memset(warm_in[:], 0.0)
        for pos in range(4):
            nc.scalar.dma_start(
                out=bpad[0:1, pos * HID : (pos + 1) * HID], in_=b_in[pos].rearrange("(o c) -> o c", o=1)
            )
        nc.scalar.activation(out=warm_out[:], in_=warm_in[:], func=ACT.Sigmoid)
        make_identity(nc, ident[:])

        for kind, lo, hi in LOADS:
            if kind == "w":
                nc.sync.dma_start(
                    out=wraw[:, lo, :].rearrange("p (j r) -> p j r", j=4),
                    in_=w_in[lo].rearrange("(j q e) c -> q j (e c)", j=4, q=P, e=2),
                )
            elif kind == "u":
                for pos in range(4):
                    nc.sync.dma_start(out=usb[:, pos, :, :], in_=u_in[pos].rearrange("(q e) c -> q e c", e=2))
            elif kind == "h":
                nc.sync.dma_start(out=hs[:, lo:hi, :], in_=hv[:, lo:hi, :])
            elif kind == "c":
                nc.sync.dma_start(out=cs[:, lo:hi, :], in_=cv[:, lo:hi, :])
            else:
                nc.sync.dma_start(out=xs[lo // 4][:, lo % 4 : lo % 4 + hi - lo, :], in_=xv[:, lo:hi, :])

        tiles = {}
        queue = {"t": [], "s": [], "v": [], "g": []}

        def put(engine, when, key, needs, emit, alloc=()):
            queue[engine].append((when, len(queue[engine]), key, list(needs), emit, alloc))

        def sb(tag, key, shape, dtype):
            tiles[key] = work.tile(shape, dtype, name=tag, bufs=BUFS[tag], align_bytes=64)

        def ps(tag, key, shape):
            tiles[key] = psum.tile(shape, F32, name=tag, bufs=BUFS[tag])

        def cols_of(half):
            return slice(half * HALF, (half + 1) * HALF)

        def gate_view(t, cols):
            return tiles[("gt", t // 2)][:, t % 2, cols]

        def bias_matmul(half):
            ps("hu", ("bb", half), [P, HALF])
            nc.tensor.matmul(out=tiles[("bb", half)][:], lhsT=ones[:], rhs=bpad[:, cols_of(half)], start=True, stop=True)

        def bias_exit(half):
            nc.scalar.copy(out=bias_bc[:, cols_of(half)], in_=tiles[("bb", half)][:])

        for half in range(2):
            put("t", VT["BB"], ("BB", half), (), lambda half=half: bias_matmul(half), (("hu", ("BBX", half)),))
            put("s", VT["BB"], ("BBX", half), (("BB", half),), lambda half=half: bias_exit(half))

        def w_regroup(pos, g):
            half, a = pos // 2, pos % 2
            if a == 0:
                sb("wg", ("wg", half, g), [P, 4 * HALF], BF16)
            src = wraw[:, pos, g * IN : (g + 1) * IN].rearrange("p (t c i) -> p c t i", t=4, i=4)
            dst = tiles[("wg", half, g)][:, a * IN : (a + 1) * IN].rearrange("p (c i t) -> p c t i", i=4, t=4)
            if W_ENG[2 * pos + g] == "v":
                nc.vector.tensor_copy(out=dst, in_=src)
            else:
                nc.scalar.copy(out=dst, in_=src)

        def w_quant(half, g):
            nc.vector.quantize_mx(
                out=wc[:, half, g, :].bitcast(FP8X4), scales=wsc[:, half, g, :], in_=tiles[("wg", half, g)][:]
            )

        for pos in range(4):
            for g in range(2):
                needs = [("WR", pos - 1, g)] if pos % 2 else ([("WQ", 0, g)] if pos == 2 else [])
                put(
                    W_ENG[2 * pos + g], VT["WR"][pos // 2] + 0.1 * (pos % 2) + 0.01 * g, ("WR", pos, g), needs,
                    lambda pos=pos, g=g: w_regroup(pos, g),
                )
        for half in range(2):
            for g in range(2):
                put(
                    "v", VT["WQ"][half] + 0.01 * g, ("WQ", half, g), (("WR", 2 * half, g), ("WR", 2 * half + 1, g)),
                    lambda half=half, g=g: w_quant(half, g),
                )

        def h_transpose(q, i):
            if i == 0:
                ps("tr", ("trh", q), [P, 4, P])
            nc.tensor.transpose(
                out=tiles[("trh", q)][:, i, :], in_=hs[:, 4 * q + i, :].bitcast(F32), identity=ident[:]
            )

        def h_exit(q):
            sb("hT", ("hT", q), [P, 4, P], F32)
            nc.scalar.copy(out=tiles[("hT", q)][:], in_=tiles[("trh", q)][:])

        def x_transpose(t, j):
            if j == 0:
                ps("tr", ("trx", t), [P, 4, P])
            words = xs[t // 4][:, t % 4, :].bitcast(F32)
            nc.tensor.transpose(out=tiles[("trx", t)][:, j, :], in_=words[:, j * P : (j + 1) * P], identity=ident[:])

        def x_exit(t):
            if t % 2 == 0:
                sb("xg", ("xg", t // 2), [P, 2, IN], BF16)
            nc.scalar.copy(
                out=tiles[("xg", t // 2)][:, t % 2, :].bitcast(F32).rearrange("p (g b u) -> p g b u", g=2, u=2),
                in_=tiles[("trx", t)][:].rearrange("p (g u) b -> p g b u", g=2),
            )

        def x_quant(j):
            sb("xc", ("xc", j), [P, 4 * P], U32)
            tiles[("xsc", j)] = work.tile([P, 4 * P], U8, name="xsc", bufs=BUFS["xc"], align_bytes=64)
            nc.vector.quantize_mx(
                out=tiles[("xc", j)][:].bitcast(FP8X4),
                scales=tiles[("xsc", j)][:],
                in_=tiles[("xg", j)][:].rearrange("p a k -> p (a k)"),
            )

        def hu_matmul(t, half, step):
            with_bias = (t, half) in S_HALVES
            if step == (-1 if with_bias else 0):
                if t % 2 == 0 and half == 0:
                    sb("gt", ("gt", t // 2), [P, 2, GATES], F32)
                ps("hu", ("hu", t, half), [P, HALF])
            acc = tiles[("hu", t, half)]
            if step < 0:
                nc.tensor.matmul(out=acc[:], lhsT=ones[:], rhs=bpad[:, cols_of(half)], start=True, stop=False)
            else:
                lhs = tiles[("hT", t // 4)][:, t % 4, :].bitcast(BF16).rearrange("p (b e) -> p b e", e=2)
                nc.tensor.matmul(
                    out=acc[:].rearrange("p (a c) -> p a c", a=2),
                    lhsT=lhs[:, :, step],
                    rhs=usb[:, 2 * half : 2 * half + 2, step, :],
                    start=(step == 0 and not with_bias),
                    stop=(step == 1),
                )

        def hu_exit(t, half):
            if (t, half) in S_HALVES:
                nc.scalar.copy(out=gate_view(t, cols_of(half)), in_=tiles[("hu", t, half)][:])
            else:
                nc.vector.tensor_tensor(
                    out=gate_view(t, cols_of(half)), in0=tiles[("hu", t, half)][:], in1=bias_bc[:, cols_of(half)],
                    op=ALU.add,
                )

        def mx_pass(t, half, g):
            if g == 0:
                ps("xw", ("xw", t, half), [P, HALF])
            rows = slice((2 * (t % 2) + g) * P, (2 * (t % 2) + g + 1) * P)
            nc.tensor.matmul_mx(
                out=tiles[("xw", t, half)][:],
                lhsT=tiles[("xc", t // 2)][:, rows].bitcast(FP8X4),
                lhsT_scale=tiles[("xsc", t // 2)][:, rows],
                rhs=wc[:, half, g, :].bitcast(FP8X4),
                rhs_scale=wsc[:, half, g, :],
                start=(g == 0),
                stop=(g == 1),
            )

        def add_xw(t, half):
            view = gate_view(t, cols_of(half))
            nc.vector.tensor_tensor(out=view, in0=tiles[("xw", t, half)][:], in1=view, op=ALU.add)

        def gate_functions(t, half):
            if half == 0:
                view = gate_view(t, slice(0, 2 * HID))
                nc.scalar.activation(out=view, in_=view, func=ACT.Sigmoid)
            else:
                view = gate_view(t, slice(2 * HID, 3 * HID))
                nc.scalar.activation(out=view, in_=view, func=ACT.Sigmoid)
                view = gate_view(t, slice(3 * HID, GATES))
                nc.scalar.activation(out=view, in_=view, func=ACT.Tanh)

        def cell_op(eng, j, lo, hi, n):
            g = tiles[("gt", j)]
            if n == 0 and lo == 0:
                sb("ta", ("ta", j), [P, 2, HID], F32)
            if n == 1 and lo == 0:
                sb("tb", ("tb", j), [P, 2, HID], F32)
            a, b = tiles[("ta", j)][:, lo:hi, :], (tiles[("tb", j)][:, lo:hi, :] if n in (1, 2) else None)
            if n == 0:
                eng.tensor_tensor(out=a, in0=g[:, lo:hi, 0:HID], in1=cs[:, 2 * j + lo : 2 * j + hi, :], op=ALU.mult)
            elif n == 1:
                eng.tensor_tensor(out=b, in0=g[:, lo:hi, HID : 2 * HID], in1=g[:, lo:hi, 3 * HID : GATES], op=ALU.mult)
            elif n == 2:
                eng.tensor_tensor(out=a, in0=a, in1=b, op=ALU.add)
            elif n == 3:
                nc.scalar.activation(out=a, in_=a, func=ACT.Tanh)
            else:
                if lo == 0:
                    sb("ot", ("ot", j), [P, 2, HID], F32)
                o = tiles[("ot", j)][:, lo:hi, :]
                eng.tensor_tensor(out=o, in0=g[:, lo:hi, 2 * HID : 3 * HID], in1=a, op=ALU.mult)
                nc.sync.dma_start(out=ov[:, 2 * j + lo : 2 * j + hi, :], in_=o)

        for s in range(-8, NT):
            mms, trs = [], []
            for t in [t for t in range(NT) if t - lead(t) == s]:
                for half in range(2):
                    first = -1 if (t, half) in S_HALVES else 0
                    for step in range(first, 2):
                        alloc = ()
                        if step == first:
                            alloc = (("hu", ("C", t, half)),)
                            if t % 2 == 0 and half == 0:
                                alloc = alloc + (("gt", ("CELL", t // 2, 1, 4)),)
                        mms.append((("H", t, half, step), (("HE", t // 4),), lambda t=t, half=half, step=step: hu_matmul(t, half, step), alloc))
            for t in [t for t in range(NT) if xslot(t) == s]:
                for j in range(4):
                    trs.append((("TRX", t, j), (), lambda t=t, j=j: x_transpose(t, j), (("tr", ("XE", t)),) if j == 0 else ()))
            for t in [t for t in range(0, NT, 4) if t - lead(t) - 2 == s]:
                for i in range(4):
                    trs.append((("TRH", t // 4, i), (), lambda q=t // 4, i=i: h_transpose(q, i), (("tr", ("HE", t // 4)),) if i == 0 else ()))
            order = []
            if not mms:
                order = trs
            elif T_ORDER == "mid":
                order = mms[: len(mms) // 2] + trs + mms[len(mms) // 2 :]
            elif T_ORDER == "front":
                order = trs + mms
            elif T_ORDER == "back":
                order = mms + trs
            else:
                k, gaps = 0, len(mms) - 1
                for i, mm in enumerate(mms):
                    order.append(mm)
                    if i < gaps:
                        share = -((k - len(trs)) // (gaps - i))
                        order.extend(trs[k : k + share])
                        k += share
            for key, needs, emit, alloc in order:
                put("t", s, key, needs, emit, alloc)
            if 0 <= s:
                for half in range(2):
                    for g in range(2):
                        put(
                            "t", s, ("M", s, half, g), (("Q", s // 2), ("WQ", half, g)),
                            lambda s=s, half=half, g=g: mx_pass(s, half, g),
                            (("xw", ("D", s, half)),) if g == 0 else (),
                        )

        for q in range(NT // 4):
            put("s", 4 * q - lead(4 * q) + VT["HE"], ("HE", q), (("TRH", q, 3),), lambda q=q: h_exit(q), (("hT", ("H", 4 * q + 3, 1, 1)),))
        for t in range(NT):
            put("s", xslot(t) + VT["XE"], ("XE", t), (("TRX", t, 3),), lambda t=t: x_exit(t), (("xg", ("Q", t // 2)),) if t % 2 == 0 else ())
            for half in range(2):
                on_s = (t, half) in S_HALVES
                put(
                    "s" if on_s else "v", t - lead(t) + (VT["CS"] if on_s else VT["C"]) + 0.01 * half, ("C", t, half),
                    (("H", t, half, 1),) + (() if on_s else (("BBX", half),)), lambda t=t, half=half: hu_exit(t, half),
                )
                put("v", t + VT["D"] + 0.1 * half, ("D", t, half), (("M", t, half, 1), ("C", t, half)), lambda t=t, half=half: add_xw(t, half))
                put("s", t + (VT["ACT0"], VT["ACT1"])[half], ("ACT", t, half), (("D", t, half),), lambda t=t, half=half: gate_functions(t, half))
        for j in range(NPAIR):
            put("v", QVT0[j] if j < len(QVT0) else 2 * j + VT["Q"], ("Q", j), (("XE", 2 * j), ("XE", 2 * j + 1)), lambda j=j: x_quant(j), (("xc", ("M", 2 * j + 1, 1, 1)),))
            parts = ((0, 1), (1, 2)) if j in V_PAIRS else ((0, 2),)
            for lo, hi in parts:
                last = hi - 1
                for n in range(5):
                    on_g = n != 3 and ((n if n < 3 else 3) < G_OPS or j in G4_PAIRS) and j not in V_PAIRS
                    engine = "s" if n == 3 else ("g" if on_g else "v")
                    eng = nc.gpsimd if on_g else nc.vector
                    needs = [("CELL", j, last, n - 1)] if n > 1 else []
                    if n == 0:
                        needs = [("ACT", 2 * j + i, 0) for i in range(lo, hi)] + ([("CELL", j - 1, 1, 0)] if j else [])
                    if n == 1:
                        needs = [("ACT", 2 * j + i, h) for i in range(lo, hi) for h in range(2)] + [("CELL", j, last, 0)]
                    when = 2 * j + (VT["TC"] if n == 3 else (VT["O"] if n == 4 else VT["CELL"] + 0.001 * n))
                    if j in V_PAIRS:
                        when = 2 * j + last + (TAIL["TC"] if n == 3 else (TAIL["O"] if n == 4 else TAIL["cell"] + 0.001 * n))
                    put(engine, when, ("CELL", j, last, n), needs, lambda eng=eng, j=j, lo=lo, hi=hi, n=n: cell_op(eng, j, lo, hi, n))

        rings, lists = {}, {}
        for engine in ("t", "s", "v", "g"):
            lists[engine] = sorted(queue[engine], key=lambda item: (item[0], item[1]))
            for item in lists[engine]:
                for tag, release in item[5]:
                    ring = rings.get(tag, [])
                    if len(ring) >= BUFS[tag]:
                        item[3].append(ring[len(ring) - BUFS[tag]])
                    rings[tag] = ring + [release]
        written = set()
        at = {"t": 0, "s": 0, "v": 0, "g": 0}
        moved = True
        while moved:
            moved = False
            for engine in ("t", "s", "v", "g"):
                while at[engine] < len(lists[engine]) and all([k in written for k in lists[engine][at[engine]][3]]):
                    item = lists[engine][at[engine]]
                    item[4]()
                    written.add(item[2])
                    at[engine] += 1
                    moved = True
        assert all([at[e] == len(lists[e]) for e in at]), "the queues wait for each other: %s" % str(
            [(lists[e][at[e]][2], [k for k in lists[e][at[e]][3] if k not in written]) for e in at if at[e] < len(lists[e])]
        )
